import numpy as np
import ml_dtypes


def mxq(x, axis, fmt="e4m3"):
    dtype, down = {"e4m3": (ml_dtypes.float8_e4m3fn, 7), "e5m2": (ml_dtypes.float8_e5m2, 14)}[fmt]
    v = np.moveaxis(np.asarray(x, np.float32).astype(ml_dtypes.bfloat16).astype(np.float64), axis, -1)
    blocks = v.reshape(v.shape[:-1] + (-1, 32))
    amax = np.abs(blocks).max(-1, keepdims=True)
    byte = np.maximum(np.where(amax > 0, np.frexp(amax)[1] - 1 + 127, 0) - down, 1)
    scale = np.exp2(byte - 127.0)
    codes = (blocks / scale).astype(np.float32).astype(dtype).astype(np.float64)
    return np.moveaxis((codes * scale).reshape(v.shape), -1, axis)


WIDE = False


def mx_kscale(k):
    if not WIDE:
        return np.ones(k)
    levels = np.array([10, -10, 5, -5, 0])
    a = np.random.permutation(np.resize(levels, k // 512 * 4)).reshape(k // 512, 4)
    idx = np.arange(k)
    return np.exp2(a[idx // 512, idx % 128 // 32])


BF16 = ml_dtypes.bfloat16


def bf(x):
    return np.asarray(x, np.float32).astype(BF16)


def f64(x):
    return np.asarray(x).astype(np.float64)


E2M1 = np.array([0.0, 0.5, 1.0, 1.5, 2.0, 3.0, 4.0, 6.0, -0.0, -0.5, -1.0, -1.5, -2.0, -3.0, -4.0, -6.0])


def pack_weight(w, fmt):
    k, n = w.shape
    w = f64(bf(w)).reshape(k // 32, 32, n)
    amax = np.abs(w).max(1)
    if fmt == "e4m3":
        byte = np.frexp(amax)[1] - 1 + 127 - 7
    else:
        mant, ex = np.frexp(amax / 6.0)
        byte = np.where(mant > 0.5, ex, ex - 1) + 127
    byte = np.clip(np.where(amax > 0, byte, 1), 1, 254)
    scaled = (w * np.exp2(127.0 - byte)[:, None, :]).reshape(k, n).astype(np.float32)
    by_word = np.ascontiguousarray(scaled.reshape(k // 512, 128, 4, n).transpose(0, 1, 3, 2))
    if fmt == "e4m3":
        words = by_word.astype(ml_dtypes.float8_e4m3fn).view(np.uint8)
    else:
        c = by_word.astype(ml_dtypes.float4_e2m1fn).view(np.uint8) & 0xF
        words = c[..., 0::2] | (c[..., 1::2] << 4)
    return np.ascontiguousarray(words), np.ascontiguousarray(byte.astype(np.uint8).reshape(k // 512, 16, n))


def unpack_weight(words, scales, fmt):
    g, p, n, _ = words.shape
    if fmt == "e4m3":
        vals = np.ascontiguousarray(words).view(ml_dtypes.float8_e4m3fn).astype(np.float64)
    else:
        nib = np.empty((g, p, n, 4), np.uint8)
        nib[..., 0::2] = words & 0xF
        nib[..., 1::2] = words >> 4
        vals = E2M1[nib]
    vals = vals * np.repeat(np.exp2(scales.astype(np.float64) - 127.0), 8, axis=1)[..., None]
    return vals.transpose(0, 1, 3, 2).reshape(g * 512, n)


B, D, H = 256, 8192, 1024
M_SCALE = 1.5
FMT = "e4m3"


def setup_inputs():
    s, t = mx_kscale(D), mx_kscale(H)
    x = bf(np.random.standard_normal((B, D)) * s)
    h_prev = bf(np.random.standard_normal((B, H)) * t)
    c_prev = bf(np.random.standard_normal((B, H)))
    W_ih = np.random.standard_normal((2 * H, D)) * 0.7 / np.sqrt(D) / s[None, :]
    b_ih = bf(np.random.standard_normal(2 * H) * 0.2)
    W_hh = np.random.standard_normal((2 * H, H)) * 0.7 / np.sqrt(H) / t[None, :]
    b_hh = bf(np.random.standard_normal(2 * H) * 0.2)
    log_lambda = bf(np.log(np.random.uniform(0.05, 0.5, H)))
    z_bias = bf(np.random.standard_normal(H) * 0.2)
    m_bias = bf(np.random.standard_normal(H) * 0.2)
    W_ih_words, W_ih_scales = pack_weight(np.ascontiguousarray(W_ih.T), FMT)
    W_hh_words, W_hh_scales = pack_weight(np.ascontiguousarray(W_hh.T), FMT)
    return {'x': x,
            'h_prev': h_prev,
            'c_prev': c_prev,
            'W_ih_words': W_ih_words,
            'W_ih_scales': W_ih_scales,
            'b_ih': b_ih,
            'W_hh_words': W_hh_words,
            'W_hh_scales': W_hh_scales,
            'b_hh': b_hh,
            'log_lambda': log_lambda,
            'z_bias': z_bias,
            'm_bias': m_bias}


def reference(x, h_prev, c_prev, W_ih_words, W_ih_scales, b_ih, W_hh_words, W_hh_scales, b_hh, log_lambda, z_bias, m_bias):
    gates = ((mxq(f64(x), 1, 'e4m3') @ unpack_weight(W_ih_words, W_ih_scales, FMT)) + f64(b_ih)
             + (mxq(f64(h_prev), 1, 'e4m3') @ unpack_weight(W_hh_words, W_hh_scales, FMT)) + f64(b_hh))
    z_raw, m_raw = gates[:, :H], gates[:, H:]
    z_t = np.tanh(z_raw + f64(z_bias))
    M_t = M_SCALE * np.tanh(m_raw + f64(m_bias))
    A_base = -np.exp(f64(log_lambda))
    innov = z_t - M_t * (A_base * f64(c_prev))
    return z_t, M_t, innov

@@ -1,0 +1,212 @@
+from contextlib import ExitStack
+
+import concourse.mybir as mybir
+from concourse.masks import make_identity
+
+BF16 = mybir.dt.bfloat16
+F32 = mybir.dt.float32
+I32 = mybir.dt.int32
+U32 = mybir.dt.uint32
+U8 = mybir.dt.uint8
+FP8X4 = mybir.dt.float8_e4m3fn_x4
+ADD = mybir.AluOpType.add
+MULT = mybir.AluOpType.mult
+TANH = mybir.ActivationFunctionType.Tanh
+EXP = mybir.ActivationFunctionType.Exp
+
+P = 128
+B, D, H = 256, 8192, 1024
+M_SCALE = 1.5
+ROW_TILES = B // P
+K_PASS = 4 * P
+WORDS_PASS = K_PASS // 2
+X_PASSES = D // K_PASS
+PASSES = (D + H) // K_PASS
+BANK = 512
+HALF_BANKS = H // BANK
+X_CHUNK = 2048
+PLANES_PER_SLOT = 4
+PLANE_SLOTS = 5
+W_BUFS = 16
+Z_HALF = 0
+M_HALF = 1
+
+FLOPS = 2 * B * (D + H) * 2 * H
+
+
+def tile_koslmcell_pa_k_kernel(
+    tc,
+    x,
+    h_prev,
+    c_prev,
+    W_ih_words,
+    W_ih_scales,
+    b_ih,
+    W_hh_words,
+    W_hh_scales,
+    b_hh,
+    log_lambda,
+    z_bias,
+    m_bias,
+    out_0,
+    out_1,
+    out_2,
+):
+    nc = tc.nc
+    with ExitStack() as ctx:
+        keep = ctx.enter_context(tc.tile_pool(name="keep", bufs=1))
+        stage = ctx.enter_context(tc.tile_pool(name="stage", bufs=4))
+        weights = ctx.enter_context(tc.tile_pool(name="weights", bufs=W_BUFS))
+        psum = ctx.enter_context(tc.psum_pool(name="psum", bufs=8))
+
+        ident = keep.tile([P, P], F32)
+        make_identity(nc, ident[:])
+        ones = keep.tile([P, P], BF16)
+        nc.vector.memset(ones[:], 1.0)
+
+        vec_rows = keep.tile([P, 3 * H], BF16)
+        nc.vector.memset(vec_rows[:], 0.0)
+        nc.scalar.dma_start(out=vec_rows[0:1, 0 : 2 * H], in_=b_ih.rearrange("(o n) -> o n", o=1))
+        nc.scalar.dma_start(out=vec_rows[1:2, 0 : 2 * H], in_=b_hh.rearrange("(o n) -> o n", o=1))
+        nc.scalar.dma_start(out=vec_rows[2:3, 0:H], in_=z_bias.rearrange("(o n) -> o n", o=1))
+        nc.scalar.dma_start(out=vec_rows[2:3, H : 2 * H], in_=m_bias.rearrange("(o n) -> o n", o=1))
+        nc.scalar.dma_start(out=vec_rows[0:1, 2 * H : 3 * H], in_=log_lambda.rearrange("(o n) -> o n", o=1))
+
+        x_sb = keep.tile([P, ROW_TILES, D], BF16)
+        x_rows = x.rearrange("(m p) k -> p m k", p=P)
+        for c0 in range(0, D, X_CHUNK):
+            nc.sync.dma_start(out=x_sb[:, :, c0 : c0 + X_CHUNK], in_=x_rows[:, :, c0 : c0 + X_CHUNK])
+        h_sb = keep.tile([P, ROW_TILES, H], BF16)
+        nc.sync.dma_start(out=h_sb[:], in_=h_prev.rearrange("(m p) k -> p m k", p=P))
+        c_sb = keep.tile([P, ROW_TILES, H], BF16)
+        nc.sync.dma_start(out=c_sb[:], in_=c_prev.rearrange("(m p) k -> p m k", p=P))
+
+        w_planes = keep.tile([P, PLANE_SLOTS, 2 * H], U8, align_bytes=64)
+        nc.vector.memset(w_planes[:].bitcast(I32), 0)
+        for slot in range(X_PASSES // PLANES_PER_SLOT):
+            g0 = slot * PLANES_PER_SLOT
+            for quad in range(4):
+                nc.sync.dma_start(
+                    out=w_planes[32 * quad : 32 * quad + 16, slot, :].bitcast(I32),
+                    in_=W_ih_scales[g0 : g0 + PLANES_PER_SLOT, 4 * quad : 4 * quad + 4, :].bitcast(I32),
+                )
+        for quad in range(4):
+            nc.sync.dma_start(
+                out=w_planes[32 * quad : 32 * quad + 8, PLANE_SLOTS - 1, :].bitcast(I32),
+                in_=W_hh_scales[:, 4 * quad : 4 * quad + 4, :].bitcast(I32),
+            )
+
+        def load_weight_words(half, g):
+            w_words = weights.tile([P, H], U32, align_bytes=64)
+            source = W_ih_words[g] if g < X_PASSES else W_hh_words[g - X_PASSES]
+            source = source.rearrange("p n t -> p (n t)")[:, 4 * H * half : 4 * H * (half + 1)]
+            nc.sync.dma_start(out=w_words[:].bitcast(I32), in_=source.bitcast(I32))
+            return w_words
+
+        chunks = [(half, g) for half in (M_HALF, Z_HALF) for g in range(PASSES)]
+        w_tiles = {}
+        for i in range(W_BUFS):
+            w_tiles[i] = load_weight_words(chunks[i][0], chunks[i][1])
+
+        x_codes = keep.tile([P, PASSES, B], U32, align_bytes=64)
+        x_planes = keep.tile([P, PASSES, B], U8, align_bytes=64)
+        x_words = x_sb[:].bitcast(F32)
+        h_words = h_sb[:].bitcast(F32)
+
+        def quantise(g, grouped):
+            nc.vector.quantize_mx(
+                out=x_codes[:, g, :].bitcast(FP8X4), scales=x_planes[:, g, :], in_=grouped[:]
+            )
+
+        waiting = None
+        for g in range(PASSES):
+            words = x_words if g < X_PASSES else h_words
+            w0 = WORDS_PASS * (g if g < X_PASSES else g - X_PASSES)
+            flipped = psum.tile([P, 2, B], F32, tag="bank")
+            for m in range(ROW_TILES):
+                for u in range(2):
+                    nc.tensor.transpose(
+                        flipped[:, u, m * P : (m + 1) * P],
+                        words[:, m, w0 + u : w0 + WORDS_PASS : 2],
+                        ident[:],
+                    )
+            grouped = stage.tile([P, 4 * B], BF16, align_bytes=64)
+            grouped_words = grouped[:].bitcast(F32).rearrange("p (b u) -> p b u", u=2)
+            if g % 2 == 0:
+                nc.scalar.copy(out=grouped_words, in_=flipped[:].rearrange("p u b -> p b u"))
+            else:
+                nc.vector.tensor_copy(out=grouped_words, in_=flipped[:].rearrange("p u b -> p b u"))
+            if waiting is not None:
+                quantise(waiting[0], waiting[1])
+            waiting = (g, grouped)
+        quantise(waiting[0], waiting[1])
+
+        bias_all = keep.tile([P, 2 * H], F32)
+        decay = keep.tile([P, H], F32)
+        for j in range(3 * H // BANK):
+            spread = psum.tile([P, BANK], F32, tag="bank")
+            nc.tensor.matmul(
+                spread[:], lhsT=ones[:], rhs=vec_rows[:, j * BANK : (j + 1) * BANK], start=True, stop=True
+            )
+            if j < 2 * H // BANK:
+                nc.vector.tensor_copy(out=bias_all[:, j * BANK : (j + 1) * BANK], in_=spread[:])
+            else:
+                nc.scalar.activation(out=decay[:, j * BANK - 2 * H : (j + 1) * BANK - 2 * H], in_=spread[:], func=EXP)
+        gain = keep.tile([P, ROW_TILES, H], F32)
+        for m in range(ROW_TILES):
+            nc.vector.scalar_tensor_tensor(
+                out=gain[:, m, :], in0=decay[:], scalar=M_SCALE, in1=c_sb[:, m, :], op0=MULT, op1=MULT
+            )
+
+        z_t = keep.tile([P, ROW_TILES, H], F32)
+        big_m = keep.tile([P, ROW_TILES, H], F32)
+        correction = keep.tile([P, ROW_TILES, H], F32)
+        innov = keep.tile([P, ROW_TILES, H], F32)
+
+        def squash(half, m, j, acc, out):
+            biased = stage.tile([P, BANK], F32)
+            first = half * H + j * BANK
+            nc.vector.tensor_tensor(out=biased[:], in0=acc[:], in1=bias_all[:, first : first + BANK], op=ADD)
+            nc.scalar.activation(out=out, in_=biased[:], func=TANH)
+
+        banks = [(m, j) for m in range(ROW_TILES) for j in range(HALF_BANKS)]
+        for i in range(len(chunks)):
+            half, g = chunks[i]
+            if g == 0:
+                accs = {}
+                for m, j in banks:
+                    accs[(m, j)] = psum.tile([P, BANK], F32, tag="bank", name="acc")
+            first_row = 4 * (g % PLANES_PER_SLOT)
+            slot = g // PLANES_PER_SLOT
+            for m, j in banks:
+                nc.tensor.matmul_mx(
+                    out=accs[(m, j)][:],
+                    lhsT=x_codes[:, g, m * P : (m + 1) * P].bitcast(FP8X4),
+                    lhsT_scale=x_planes[:, g, m * P : (m + 1) * P],
+                    rhs=w_tiles[i][:, j * BANK : (j + 1) * BANK].bitcast(FP8X4),
+                    rhs_scale=w_planes[first_row:P, slot, half * H + j * BANK : half * H + (j + 1) * BANK],
+                    start=(g == 0),
+                    stop=(g == PASSES - 1),
+                )
+            if i + W_BUFS < len(chunks):
+                w_tiles[i + W_BUFS] = load_weight_words(chunks[i + W_BUFS][0], chunks[i + W_BUFS][1])
+
+            if half == M_HALF and g == PASSES - 1:
+                for m, j in banks:
+                    cols = slice(j * BANK, (j + 1) * BANK)
+                    squashed = stage.tile([P, BANK], F32)
+                    squash(M_HALF, m, j, accs[(m, j)], squashed[:])
+                    nc.scalar.mul(out=big_m[:, m, cols], in_=squashed[:], mul=M_SCALE)
+                    nc.vector.tensor_tensor(
+                        out=correction[:, m, cols], in0=squashed[:], in1=gain[:, m, cols], op=MULT
+                    )
+
+        for m in range(ROW_TILES):
+            nc.sync.dma_start(out=out_1[m * P : (m + 1) * P, :], in_=big_m[:, m, :])
+        for m, j in banks:
+            rows = slice(m * P, (m + 1) * P)
+            cols = slice(j * BANK, (j + 1) * BANK)
+            squash(Z_HALF, m, j, accs[(m, j)], z_t[:, m, cols])
+            nc.sync.dma_start(out=out_0[rows, cols], in_=z_t[:, m, cols])
+            nc.vector.tensor_tensor(out=innov[:, m, cols], in0=z_t[:, m, cols], in1=correction[:, m, cols], op=ADD)
+            nc.sync.dma_start(out=out_2[rows, cols], in_=innov[:, m, cols])

@@ -86,14 +86,14 @@ def tile_koslmcell_pa_k_kernel(
         for slot in range(X_PASSES // PLANES_PER_SLOT):
             g0 = slot * PLANES_PER_SLOT
             for quad in range(4):
-                nc.sync.dma_start(
-                    out=w_planes[32 * quad : 32 * quad + 16, slot, :].bitcast(I32),
-                    in_=W_ih_scales[g0 : g0 + PLANES_PER_SLOT, 4 * quad : 4 * quad + 4, :].bitcast(I32),
+                nc.gpsimd.dma_start(
+                    out=w_planes[32 * quad : 32 * quad + 16, slot, :].bitcast(F32),
+                    in_=W_ih_scales[g0 : g0 + PLANES_PER_SLOT, 4 * quad : 4 * quad + 4, :].bitcast(F32),
                 )
         for quad in range(4):
-            nc.sync.dma_start(
-                out=w_planes[32 * quad : 32 * quad + 8, PLANE_SLOTS - 1, :].bitcast(I32),
-                in_=W_hh_scales[:, 4 * quad : 4 * quad + 4, :].bitcast(I32),
+            nc.gpsimd.dma_start(
+                out=w_planes[32 * quad : 32 * quad + 8, PLANE_SLOTS - 1, :].bitcast(F32),
+                in_=W_hh_scales[:, 4 * quad : 4 * quad + 4, :].bitcast(F32),
             )
 
         def load_weight_words(half, g):

@@ -24,12 +24,15 @@ X_PASSES = D // K_PASS
 PASSES = (D + H) // K_PASS
 BANK = 512
 HALF_BANKS = H // BANK
+GATE_BANKS = 2 * HALF_BANKS
+PSUM_BANKS = 8
 X_CHUNK = 2048
+X_CHUNKS = D // X_CHUNK
 PLANES_PER_SLOT = 4
 PLANE_SLOTS = 5
-W_BUFS = 16
-Z_HALF = 0
-M_HALF = 1
+TAPER_PASSES = 4
+BODY_PASSES = PASSES - TAPER_PASSES
+STREAM_BUFS = 8
 
 FLOPS = 2 * B * (D + H) * 2 * H
 
@@ -56,8 +59,10 @@ def tile_koslmcell_pa_k_kernel(
     with ExitStack() as ctx:
         keep = ctx.enter_context(tc.tile_pool(name="keep", bufs=1))
         stage = ctx.enter_context(tc.tile_pool(name="stage", bufs=4))
-        weights = ctx.enter_context(tc.tile_pool(name="weights", bufs=W_BUFS))
-        psum = ctx.enter_context(tc.psum_pool(name="psum", bufs=8))
+        stream = ctx.enter_context(tc.tile_pool(name="stream", bufs=STREAM_BUFS))
+        taper = ctx.enter_context(tc.tile_pool(name="taper", bufs=TAPER_PASSES * GATE_BANKS))
+        psum = ctx.enter_context(tc.psum_pool(name="psum", bufs=PSUM_BANKS))
+        ctx.enter_context(tc.manual_schedule())
 
         ident = keep.tile([P, P], F32)
         make_identity(nc, ident[:])
@@ -72,46 +77,57 @@ def tile_koslmcell_pa_k_kernel(
         nc.scalar.dma_start(out=vec_rows[2:3, H : 2 * H], in_=m_bias.rearrange("(o n) -> o n", o=1))
         nc.scalar.dma_start(out=vec_rows[0:1, 2 * H : 3 * H], in_=log_lambda.rearrange("(o n) -> o n", o=1))
 
-        x_sb = keep.tile([P, ROW_TILES, D], BF16)
         x_rows = x.rearrange("(m p) k -> p m k", p=P)
-        for c0 in range(0, D, X_CHUNK):
-            nc.sync.dma_start(out=x_sb[:, :, c0 : c0 + X_CHUNK], in_=x_rows[:, :, c0 : c0 + X_CHUNK])
+        x_chunks = []
+        for c in range(X_CHUNKS):
+            x_chunk = stream.tile([P, ROW_TILES, X_CHUNK], BF16, tag="ring", align_bytes=64)
+            nc.sync.dma_start(out=x_chunk[:], in_=x_rows[:, :, c * X_CHUNK : (c + 1) * X_CHUNK])
+            x_chunks.append(x_chunk)
         h_sb = keep.tile([P, ROW_TILES, H], BF16)
         nc.sync.dma_start(out=h_sb[:], in_=h_prev.rearrange("(m p) k -> p m k", p=P))
-        c_sb = keep.tile([P, ROW_TILES, H], BF16)
-        nc.sync.dma_start(out=c_sb[:], in_=c_prev.rearrange("(m p) k -> p m k", p=P))
 
         w_planes = keep.tile([P, PLANE_SLOTS, 2 * H], U8, align_bytes=64)
         nc.vector.memset(w_planes[:].bitcast(I32), 0)
         for slot in range(X_PASSES // PLANES_PER_SLOT):
             g0 = slot * PLANES_PER_SLOT
             for quad in range(4):
-                nc.gpsimd.dma_start(
-                    out=w_planes[32 * quad : 32 * quad + 16, slot, :].bitcast(F32),
-                    in_=W_ih_scales[g0 : g0 + PLANES_PER_SLOT, 4 * quad : 4 * quad + 4, :].bitcast(F32),
+                nc.sync.dma_start(
+                    out=w_planes[32 * quad : 32 * quad + 16, slot, :].bitcast(I32),
+                    in_=W_ih_scales[g0 : g0 + PLANES_PER_SLOT, 4 * quad : 4 * quad + 4, :].bitcast(I32),
                 )
         for quad in range(4):
-            nc.gpsimd.dma_start(
-                out=w_planes[32 * quad : 32 * quad + 8, PLANE_SLOTS - 1, :].bitcast(F32),
-                in_=W_hh_scales[:, 4 * quad : 4 * quad + 4, :].bitcast(F32),
+            nc.sync.dma_start(
+                out=w_planes[32 * quad : 32 * quad + 8, PLANE_SLOTS - 1, :].bitcast(I32),
+                in_=W_hh_scales[:, 4 * quad : 4 * quad + 4, :].bitcast(I32),
             )
 
-        def load_weight_words(half, g):
-            w_words = weights.tile([P, H], U32, align_bytes=64)
+        def weight_bytes(g):
             source = W_ih_words[g] if g < X_PASSES else W_hh_words[g - X_PASSES]
-            source = source.rearrange("p n t -> p (n t)")[:, 4 * H * half : 4 * H * (half + 1)]
-            nc.sync.dma_start(out=w_words[:].bitcast(I32), in_=source.bitcast(I32))
-            return w_words
+            return source.rearrange("p n t -> p (n t)")
 
-        chunks = [(half, g) for half in (M_HALF, Z_HALF) for g in range(PASSES)]
-        w_tiles = {}
-        for i in range(W_BUFS):
-            w_tiles[i] = load_weight_words(chunks[i][0], chunks[i][1])
+        w_whole_tiles = []
+
+        def load_whole_passes(end):
+            for g in range(len(w_whole_tiles), min(end, BODY_PASSES)):
+                w_whole = stream.tile([P, 2 * H], U32, tag="ring", align_bytes=64)
+                nc.sync.dma_start(out=w_whole[:].bitcast(I32), in_=weight_bytes(g).bitcast(I32))
+                w_whole_tiles.append(w_whole)
+
+        def load_one_bank(g, bank):
+            w_bank = taper.tile([P, BANK], U32, align_bytes=64)
+            nc.sync.dma_start(
+                out=w_bank[:].bitcast(I32),
+                in_=weight_bytes(g)[:, 4 * BANK * bank : 4 * BANK * (bank + 1)].bitcast(I32),
+            )
+            return w_bank
+
+        load_whole_passes(STREAM_BUFS - X_CHUNKS)
+        c_sb = keep.tile([P, ROW_TILES, H], BF16)
+        nc.sync.dma_start(out=c_sb[:], in_=c_prev.rearrange("(m p) k -> p m k", p=P))
 
         x_codes = keep.tile([P, PASSES, B], U32, align_bytes=64)
         x_planes = keep.tile([P, PASSES, B], U8, align_bytes=64)
-        x_words = x_sb[:].bitcast(F32)
-        h_words = h_sb[:].bitcast(F32)
+        passes_per_chunk = X_CHUNK // K_PASS
 
         def quantise(g, grouped):
             nc.vector.quantize_mx(
@@ -120,8 +136,12 @@ def tile_koslmcell_pa_k_kernel(
 
         waiting = None
         for g in range(PASSES):
-            words = x_words if g < X_PASSES else h_words
-            w0 = WORDS_PASS * (g if g < X_PASSES else g - X_PASSES)
+            if g < X_PASSES:
+                words = x_chunks[g // passes_per_chunk][:].bitcast(F32)
+                w0 = WORDS_PASS * (g % passes_per_chunk)
+            else:
+                words = h_sb[:].bitcast(F32)
+                w0 = WORDS_PASS * (g - X_PASSES)
             flipped = psum.tile([P, 2, B], F32, tag="bank")
             for m in range(ROW_TILES):
                 for u in range(2):
@@ -140,6 +160,7 @@ def tile_koslmcell_pa_k_kernel(
                 quantise(waiting[0], waiting[1])
             waiting = (g, grouped)
         quantise(waiting[0], waiting[1])
+        load_whole_passes(STREAM_BUFS)
 
         bias_all = keep.tile([P, 2 * H], F32)
         decay = keep.tile([P, H], F32)
@@ -148,7 +169,7 @@ def tile_koslmcell_pa_k_kernel(
             nc.tensor.matmul(
                 spread[:], lhsT=ones[:], rhs=vec_rows[:, j * BANK : (j + 1) * BANK], start=True, stop=True
             )
-            if j < 2 * H // BANK:
+            if j < GATE_BANKS:
                 nc.vector.tensor_copy(out=bias_all[:, j * BANK : (j + 1) * BANK], in_=spread[:])
             else:
                 nc.scalar.activation(out=decay[:, j * BANK - 2 * H : (j + 1) * BANK - 2 * H], in_=spread[:], func=EXP)
@@ -158,55 +179,66 @@ def tile_koslmcell_pa_k_kernel(
                 out=gain[:, m, :], in0=decay[:], scalar=M_SCALE, in1=c_sb[:, m, :], op0=MULT, op1=MULT
             )
 
+        accs = {}
+        for m in range(ROW_TILES):
+            for bank in range(GATE_BANKS):
+                accs[(m, bank)] = psum.tile([P, BANK], F32, tag="bank", name="acc")
+
+        def mx_pass(g, m, bank, w_cols):
+            first_row = 4 * (g % PLANES_PER_SLOT)
+            nc.tensor.matmul_mx(
+                out=accs[(m, bank)][:],
+                lhsT=x_codes[:, g, m * P : (m + 1) * P].bitcast(FP8X4),
+                lhsT_scale=x_planes[:, g, m * P : (m + 1) * P],
+                rhs=w_cols.bitcast(FP8X4),
+                rhs_scale=w_planes[first_row:P, g // PLANES_PER_SLOT, bank * BANK : (bank + 1) * BANK],
+                start=(g == 0),
+                stop=(g == PASSES - 1),
+            )
+
+        for g in range(BODY_PASSES):
+            for m in range(ROW_TILES):
+                for bank in range(GATE_BANKS):
+                    mx_pass(g, m, bank, w_whole_tiles[g][:, bank * BANK : (bank + 1) * BANK])
+            load_whole_passes(g + 1 + STREAM_BUFS)
+
+        closing_order = list(range(HALF_BANKS, GATE_BANKS)) + list(range(HALF_BANKS))
+        w_bank_tiles = {}
+        for bank in closing_order:
+            for g in range(BODY_PASSES, PASSES):
+                w_bank_tiles[(g, bank)] = load_one_bank(g, bank)
+
         z_t = keep.tile([P, ROW_TILES, H], F32)
+        tanh_m = keep.tile([P, ROW_TILES, H], F32)
         big_m = keep.tile([P, ROW_TILES, H], F32)
         correction = keep.tile([P, ROW_TILES, H], F32)
         innov = keep.tile([P, ROW_TILES, H], F32)
 
-        def squash(half, m, j, acc, out):
-            biased = stage.tile([P, BANK], F32)
-            first = half * H + j * BANK
-            nc.vector.tensor_tensor(out=biased[:], in0=acc[:], in1=bias_all[:, first : first + BANK], op=ADD)
-            nc.scalar.activation(out=out, in_=biased[:], func=TANH)
-
-        banks = [(m, j) for m in range(ROW_TILES) for j in range(HALF_BANKS)]
-        for i in range(len(chunks)):
-            half, g = chunks[i]
-            if g == 0:
-                accs = {}
-                for m, j in banks:
-                    accs[(m, j)] = psum.tile([P, BANK], F32, tag="bank", name="acc")
-            first_row = 4 * (g % PLANES_PER_SLOT)
-            slot = g // PLANES_PER_SLOT
-            for m, j in banks:
-                nc.tensor.matmul_mx(
-                    out=accs[(m, j)][:],
-                    lhsT=x_codes[:, g, m * P : (m + 1) * P].bitcast(FP8X4),
-                    lhsT_scale=x_planes[:, g, m * P : (m + 1) * P],
-                    rhs=w_tiles[i][:, j * BANK : (j + 1) * BANK].bitcast(FP8X4),
-                    rhs_scale=w_planes[first_row:P, slot, half * H + j * BANK : half * H + (j + 1) * BANK],
-                    start=(g == 0),
-                    stop=(g == PASSES - 1),
-                )
-            if i + W_BUFS < len(chunks):
-                w_tiles[i + W_BUFS] = load_weight_words(chunks[i + W_BUFS][0], chunks[i + W_BUFS][1])
-
-            if half == M_HALF and g == PASSES - 1:
-                for m, j in banks:
-                    cols = slice(j * BANK, (j + 1) * BANK)
-                    squashed = stage.tile([P, BANK], F32)
-                    squash(M_HALF, m, j, accs[(m, j)], squashed[:])
-                    nc.scalar.mul(out=big_m[:, m, cols], in_=squashed[:], mul=M_SCALE)
-                    nc.vector.tensor_tensor(
-                        out=correction[:, m, cols], in0=squashed[:], in1=gain[:, m, cols], op=MULT
-                    )
-
-        for m in range(ROW_TILES):
-            nc.sync.dma_start(out=out_1[m * P : (m + 1) * P, :], in_=big_m[:, m, :])
-        for m, j in banks:
-            rows = slice(m * P, (m + 1) * P)
+        for bank in closing_order:
+            for g in range(BODY_PASSES, PASSES):
+                for m in range(ROW_TILES):
+                    mx_pass(g, m, bank, w_bank_tiles[(g, bank)][:])
+            is_m_bank = bank >= HALF_BANKS
+            j = bank % HALF_BANKS
             cols = slice(j * BANK, (j + 1) * BANK)
-            squash(Z_HALF, m, j, accs[(m, j)], z_t[:, m, cols])
-            nc.sync.dma_start(out=out_0[rows, cols], in_=z_t[:, m, cols])
-            nc.vector.tensor_tensor(out=innov[:, m, cols], in0=z_t[:, m, cols], in1=correction[:, m, cols], op=ADD)
-            nc.sync.dma_start(out=out_2[rows, cols], in_=innov[:, m, cols])
+            squashed = tanh_m if is_m_bank else z_t
+            for m in range(ROW_TILES):
+                biased = stage.tile([P, BANK], F32)
+                nc.vector.tensor_tensor(
+                    out=biased[:], in0=accs[(m, bank)][:], in1=bias_all[:, bank * BANK : (bank + 1) * BANK], op=ADD
+                )
+                nc.scalar.activation(out=squashed[:, m, cols], in_=biased[:], func=TANH)
+            for m in range(ROW_TILES):
+                rows = slice(m * P, (m + 1) * P)
+                if is_m_bank:
+                    nc.scalar.mul(out=big_m[:, m, cols], in_=tanh_m[:, m, cols], mul=M_SCALE)
+                    nc.sync.dma_start(out=out_1[rows, cols], in_=big_m[:, m, cols])
+                    nc.vector.tensor_tensor(
+                        out=correction[:, m, cols], in0=tanh_m[:, m, cols], in1=gain[:, m, cols], op=MULT
+                    )
+                else:
+                    nc.sync.dma_start(out=out_0[rows, cols], in_=z_t[:, m, cols])
+                    nc.vector.tensor_tensor(
+                        out=innov[:, m, cols], in0=z_t[:, m, cols], in1=correction[:, m, cols], op=ADD
+                    )
+                    nc.sync.dma_start(out=out_2[rows, cols], in_=innov[:, m, cols])

@@ -66,6 +66,22 @@ def tile_koslmcell_pa_k_kernel(
 
         ident = keep.tile([P, P], F32)
         make_identity(nc, ident[:])
+
+        w_planes = keep.tile([P, PLANE_SLOTS, 2 * H], U8, align_bytes=64)
+        nc.vector.memset(w_planes[:].bitcast(I32), 0)
+        for slot in range(X_PASSES // PLANES_PER_SLOT):
+            g0 = slot * PLANES_PER_SLOT
+            for quad in range(4):
+                nc.gpsimd.dma_start(
+                    out=w_planes[32 * quad : 32 * quad + 16, slot, :].bitcast(F32),
+                    in_=W_ih_scales[g0 : g0 + PLANES_PER_SLOT, 4 * quad : 4 * quad + 4, :].bitcast(F32),
+                )
+        for quad in range(4):
+            nc.gpsimd.dma_start(
+                out=w_planes[32 * quad : 32 * quad + 8, PLANE_SLOTS - 1, :].bitcast(F32),
+                in_=W_hh_scales[:, 4 * quad : 4 * quad + 4, :].bitcast(F32),
+            )
+
         ones = keep.tile([P, P], BF16)
         nc.vector.memset(ones[:], 1.0)
 
@@ -85,21 +101,6 @@ def tile_koslmcell_pa_k_kernel(
             x_chunks.append(x_chunk)
         h_sb = keep.tile([P, ROW_TILES, H], BF16)
         nc.sync.dma_start(out=h_sb[:], in_=h_prev.rearrange("(m p) k -> p m k", p=P))
-
-        w_planes = keep.tile([P, PLANE_SLOTS, 2 * H], U8, align_bytes=64)
-        nc.vector.memset(w_planes[:].bitcast(I32), 0)
-        for slot in range(X_PASSES // PLANES_PER_SLOT):
-            g0 = slot * PLANES_PER_SLOT
-            for quad in range(4):
-                nc.sync.dma_start(
-                    out=w_planes[32 * quad : 32 * quad + 16, slot, :].bitcast(I32),
-                    in_=W_ih_scales[g0 : g0 + PLANES_PER_SLOT, 4 * quad : 4 * quad + 4, :].bitcast(I32),
-                )
-        for quad in range(4):
-            nc.sync.dma_start(
-                out=w_planes[32 * quad : 32 * quad + 8, PLANE_SLOTS - 1, :].bitcast(I32),
-                in_=W_hh_scales[:, 4 * quad : 4 * quad + 4, :].bitcast(I32),
-            )
 
         def weight_bytes(g):
             source = W_ih_words[g] if g < X_PASSES else W_hh_words[g - X_PASSES]

from contextlib import ExitStack

import concourse.mybir as mybir
from concourse.masks import make_identity

BF16 = mybir.dt.bfloat16
F32 = mybir.dt.float32
I32 = mybir.dt.int32
U32 = mybir.dt.uint32
U8 = mybir.dt.uint8
FP8X4 = mybir.dt.float8_e4m3fn_x4
ADD = mybir.AluOpType.add
MULT = mybir.AluOpType.mult
TANH = mybir.ActivationFunctionType.Tanh
EXP = mybir.ActivationFunctionType.Exp

P = 128
B, D, H = 256, 8192, 1024
M_SCALE = 1.5
ROW_TILES = B // P
K_PASS = 4 * P
WORDS_PASS = K_PASS // 2
X_PASSES = D // K_PASS
PASSES = (D + H) // K_PASS
BANK = 512
HALF_BANKS = H // BANK
GATE_BANKS = 2 * HALF_BANKS
PSUM_BANKS = 8
X_CHUNK = 2048
X_CHUNKS = D // X_CHUNK
PLANES_PER_SLOT = 4
PLANE_SLOTS = 5
TAPER_PASSES = 4
BODY_PASSES = PASSES - TAPER_PASSES
STREAM_BUFS = 8

FLOPS = 2 * B * (D + H) * 2 * H


def tile_koslmcell_pa_k_kernel(
    tc,
    x,
    h_prev,
    c_prev,
    W_ih_words,
    W_ih_scales,
    b_ih,
    W_hh_words,
    W_hh_scales,
    b_hh,
    log_lambda,
    z_bias,
    m_bias,
    out_0,
    out_1,
    out_2,
):
    nc = tc.nc
    with ExitStack() as ctx:
        keep = ctx.enter_context(tc.tile_pool(name="keep", bufs=1))
        stage = ctx.enter_context(tc.tile_pool(name="stage", bufs=4))
        stream = ctx.enter_context(tc.tile_pool(name="stream", bufs=STREAM_BUFS))
        taper = ctx.enter_context(tc.tile_pool(name="taper", bufs=TAPER_PASSES * GATE_BANKS))
        psum = ctx.enter_context(tc.psum_pool(name="psum", bufs=PSUM_BANKS))
        ctx.enter_context(tc.manual_schedule())

        ident = keep.tile([P, P], F32)
        make_identity(nc, ident[:])

        w_planes = keep.tile([P, PLANE_SLOTS, 2 * H], U8, align_bytes=64)
        nc.vector.memset(w_planes[:].bitcast(I32), 0)
        for slot in range(X_PASSES // PLANES_PER_SLOT):
            g0 = slot * PLANES_PER_SLOT
            for quad in range(4):
                nc.gpsimd.dma_start(
                    out=w_planes[32 * quad : 32 * quad + 16, slot, :].bitcast(F32),
                    in_=W_ih_scales[g0 : g0 + PLANES_PER_SLOT, 4 * quad : 4 * quad + 4, :].bitcast(F32),
                )
        for quad in range(4):
            nc.gpsimd.dma_start(
                out=w_planes[32 * quad : 32 * quad + 8, PLANE_SLOTS - 1, :].bitcast(F32),
                in_=W_hh_scales[:, 4 * quad : 4 * quad + 4, :].bitcast(F32),
            )

        ones = keep.tile([P, P], BF16)
        nc.vector.memset(ones[:], 1.0)

        vec_rows = keep.tile([P, 3 * H], BF16)
        nc.vector.memset(vec_rows[:], 0.0)
        nc.scalar.dma_start(out=vec_rows[0:1, 0 : 2 * H], in_=b_ih.rearrange("(o n) -> o n", o=1))
        nc.scalar.dma_start(out=vec_rows[1:2, 0 : 2 * H], in_=b_hh.rearrange("(o n) -> o n", o=1))
        nc.scalar.dma_start(out=vec_rows[2:3, 0:H], in_=z_bias.rearrange("(o n) -> o n", o=1))
        nc.scalar.dma_start(out=vec_rows[2:3, H : 2 * H], in_=m_bias.rearrange("(o n) -> o n", o=1))
        nc.scalar.dma_start(out=vec_rows[0:1, 2 * H : 3 * H], in_=log_lambda.rearrange("(o n) -> o n", o=1))

        x_rows = x.rearrange("(m p) k -> p m k", p=P)
        x_chunks = []
        for c in range(X_CHUNKS):
            x_chunk = stream.tile([P, ROW_TILES, X_CHUNK], BF16, tag="ring", align_bytes=64)
            nc.sync.dma_start(out=x_chunk[:], in_=x_rows[:, :, c * X_CHUNK : (c + 1) * X_CHUNK])
            x_chunks.append(x_chunk)
        h_sb = keep.tile([P, ROW_TILES, H], BF16)
        nc.sync.dma_start(out=h_sb[:], in_=h_prev.rearrange("(m p) k -> p m k", p=P))

        def weight_bytes(g):
            source = W_ih_words[g] if g < X_PASSES else W_hh_words[g - X_PASSES]
            return source.rearrange("p n t -> p (n t)")

        w_whole_tiles = []

        def load_whole_passes(end):
            for g in range(len(w_whole_tiles), min(end, BODY_PASSES)):
                w_whole = stream.tile([P, 2 * H], U32, tag="ring", align_bytes=64)
                nc.sync.dma_start(out=w_whole[:].bitcast(I32), in_=weight_bytes(g).bitcast(I32))
                w_whole_tiles.append(w_whole)

        def load_one_bank(g, bank):
            w_bank = taper.tile([P, BANK], U32, align_bytes=64)
            nc.sync.dma_start(
                out=w_bank[:].bitcast(I32),
                in_=weight_bytes(g)[:, 4 * BANK * bank : 4 * BANK * (bank + 1)].bitcast(I32),
            )
            return w_bank

        load_whole_passes(STREAM_BUFS - X_CHUNKS)
        c_sb = keep.tile([P, ROW_TILES, H], BF16)
        nc.sync.dma_start(out=c_sb[:], in_=c_prev.rearrange("(m p) k -> p m k", p=P))

        x_codes = keep.tile([P, PASSES, B], U32, align_bytes=64)
        x_planes = keep.tile([P, PASSES, B], U8, align_bytes=64)
        passes_per_chunk = X_CHUNK // K_PASS

        def quantise(g, grouped):
            nc.vector.quantize_mx(
                out=x_codes[:, g, :].bitcast(FP8X4), scales=x_planes[:, g, :], in_=grouped[:]
            )

        waiting = None
        for g in range(PASSES):
            if g < X_PASSES:
                words = x_chunks[g // passes_per_chunk][:].bitcast(F32)
                w0 = WORDS_PASS * (g % passes_per_chunk)
            else:
                words = h_sb[:].bitcast(F32)
                w0 = WORDS_PASS * (g - X_PASSES)
            flipped = psum.tile([P, 2, B], F32, tag="bank")
            for m in range(ROW_TILES):
                for u in range(2):
                    nc.tensor.transpose(
                        flipped[:, u, m * P : (m + 1) * P],
                        words[:, m, w0 + u : w0 + WORDS_PASS : 2],
                        ident[:],
                    )
            grouped = stage.tile([P, 4 * B], BF16, align_bytes=64)
            grouped_words = grouped[:].bitcast(F32).rearrange("p (b u) -> p b u", u=2)
            if g % 2 == 0:
                nc.scalar.copy(out=grouped_words, in_=flipped[:].rearrange("p u b -> p b u"))
            else:
                nc.vector.tensor_copy(out=grouped_words, in_=flipped[:].rearrange("p u b -> p b u"))
            if waiting is not None:
                quantise(waiting[0], waiting[1])
            waiting = (g, grouped)
        quantise(waiting[0], waiting[1])
        load_whole_passes(STREAM_BUFS)

        bias_all = keep.tile([P, 2 * H], F32)
        decay = keep.tile([P, H], F32)
        for j in range(3 * H // BANK):
            spread = psum.tile([P, BANK], F32, tag="bank")
            nc.tensor.matmul(
                spread[:], lhsT=ones[:], rhs=vec_rows[:, j * BANK : (j + 1) * BANK], start=True, stop=True
            )
            if j < GATE_BANKS:
                nc.vector.tensor_copy(out=bias_all[:, j * BANK : (j + 1) * BANK], in_=spread[:])
            else:
                nc.scalar.activation(out=decay[:, j * BANK - 2 * H : (j + 1) * BANK - 2 * H], in_=spread[:], func=EXP)
        gain = keep.tile([P, ROW_TILES, H], F32)
        for m in range(ROW_TILES):
            nc.vector.scalar_tensor_tensor(
                out=gain[:, m, :], in0=decay[:], scalar=M_SCALE, in1=c_sb[:, m, :], op0=MULT, op1=MULT
            )

        accs = {}
        for m in range(ROW_TILES):
            for bank in range(GATE_BANKS):
                accs[(m, bank)] = psum.tile([P, BANK], F32, tag="bank", name="acc")

        def mx_pass(g, m, bank, w_cols):
            first_row = 4 * (g % PLANES_PER_SLOT)
            nc.tensor.matmul_mx(
                out=accs[(m, bank)][:],
                lhsT=x_codes[:, g, m * P : (m + 1) * P].bitcast(FP8X4),
                lhsT_scale=x_planes[:, g, m * P : (m + 1) * P],
                rhs=w_cols.bitcast(FP8X4),
                rhs_scale=w_planes[first_row:P, g // PLANES_PER_SLOT, bank * BANK : (bank + 1) * BANK],
                start=(g == 0),
                stop=(g == PASSES - 1),
            )

        for g in range(BODY_PASSES):
            for m in range(ROW_TILES):
                for bank in range(GATE_BANKS):
                    mx_pass(g, m, bank, w_whole_tiles[g][:, bank * BANK : (bank + 1) * BANK])
            load_whole_passes(g + 1 + STREAM_BUFS)

        closing_order = list(range(HALF_BANKS, GATE_BANKS)) + list(range(HALF_BANKS))
        w_bank_tiles = {}
        for bank in closing_order:
            for g in range(BODY_PASSES, PASSES):
                w_bank_tiles[(g, bank)] = load_one_bank(g, bank)

        z_t = keep.tile([P, ROW_TILES, H], F32)
        tanh_m = keep.tile([P, ROW_TILES, H], F32)
        big_m = keep.tile([P, ROW_TILES, H], F32)
        correction = keep.tile([P, ROW_TILES, H], F32)
        innov = keep.tile([P, ROW_TILES, H], F32)

        for bank in closing_order:
            for g in range(BODY_PASSES, PASSES):
                for m in range(ROW_TILES):
                    mx_pass(g, m, bank, w_bank_tiles[(g, bank)][:])
            is_m_bank = bank >= HALF_BANKS
            j = bank % HALF_BANKS
            cols = slice(j * BANK, (j + 1) * BANK)
            squashed = tanh_m if is_m_bank else z_t
            for m in range(ROW_TILES):
                biased = stage.tile([P, BANK], F32)
                nc.vector.tensor_tensor(
                    out=biased[:], in0=accs[(m, bank)][:], in1=bias_all[:, bank * BANK : (bank + 1) * BANK], op=ADD
                )
                nc.scalar.activation(out=squashed[:, m, cols], in_=biased[:], func=TANH)
            for m in range(ROW_TILES):
                rows = slice(m * P, (m + 1) * P)
                if is_m_bank:
                    nc.scalar.mul(out=big_m[:, m, cols], in_=tanh_m[:, m, cols], mul=M_SCALE)
                    nc.sync.dma_start(out=out_1[rows, cols], in_=big_m[:, m, cols])
                    nc.vector.tensor_tensor(
                        out=correction[:, m, cols], in0=tanh_m[:, m, cols], in1=gain[:, m, cols], op=MULT
                    )
                else:
                    nc.sync.dma_start(out=out_0[rows, cols], in_=z_t[:, m, cols])
                    nc.vector.tensor_tensor(
                        out=innov[:, m, cols], in0=z_t[:, m, cols], in1=correction[:, m, cols], op=ADD
                    )
                    nc.sync.dma_start(out=out_2[rows, cols], in_=innov[:, m, cols])
